import numpy as np
import ml_dtypes


def mxq(x, axis, fmt="e4m3"):
    dtype, down = {"e4m3": (ml_dtypes.float8_e4m3fn, 7), "e5m2": (ml_dtypes.float8_e5m2, 14)}[fmt]
    v = np.moveaxis(np.asarray(x, np.float32).astype(ml_dtypes.bfloat16).astype(np.float64), axis, -1)
    blocks = v.reshape(v.shape[:-1] + (-1, 32))
    amax = np.abs(blocks).max(-1, keepdims=True)
    byte = np.maximum(np.where(amax > 0, np.frexp(amax)[1] - 1 + 127, 0) - down, 1)
    scale = np.exp2(byte - 127.0)
    codes = (blocks / scale).astype(np.float32).astype(dtype).astype(np.float64)
    return np.moveaxis((codes * scale).reshape(v.shape), -1, axis)


WIDE = False


def mx_kscale(k):
    if not WIDE:
        return np.ones(k)
    levels = np.array([10, -10, 5, -5, 0])
    a = np.random.permutation(np.resize(levels, k // 512 * 4)).reshape(k // 512, 4)
    idx = np.arange(k)
    return np.exp2(a[idx // 512, idx % 128 // 32])


BF16 = ml_dtypes.bfloat16


def bf(x):
    return np.asarray(x, np.float32).astype(BF16)


def f64(x):
    return np.asarray(x).astype(np.float64)


N, H, W, C, O, KH, KW, R = 4, 16, 16, 512, 128, 3, 3, 4
K = KH * KW * C


def patch_dot(xq, w):
    tot = np.zeros((N, H, W, O))
    for i in range(KH):
        for j in range(KW):
            t = i * KW + j
            y = (xq @ mxq(w[t * C:(t + 1) * C], 0, "e4m3")).reshape(N, H, W, O)
            yp = np.pad(y, ((0, 0), (KH // 2, KH // 2), (KW // 2, KW // 2), (0, 0)))
            tot = tot + yp[:, i:i + H, j:j + W, :]
    return tot


def cube(v):
    return v * v * v


def setup_inputs():
    s = mx_kscale(C)
    sk = np.tile(s, KH * KW)[:, None]

    def filt(scale):
        return bf(np.random.standard_normal((K, O)) * scale / sk)

    return {"x": bf(np.random.standard_normal((N, H, W, C)) * 0.8 / np.sqrt(K) * s),
            "w1": filt(1.0), "w4": filt(1.0), "w6": filt(0.6), "w7": filt(0.6), "w8": filt(0.6)}


def reference(x, w1, w4, w6, w7, w8):
    xq = mxq(f64(x).reshape(N * H * W, C), 1, "e4m3")

    def lin(w):
        return patch_dot(xq, f64(w))

    def poly(w):
        return cube(lin(w) + 1.0)

    return lin(w1), np.tanh(lin(w4)), poly(w6), poly(w7), poly(w8)

@@ -1,0 +1,274 @@
+from contextlib import ExitStack
+
+import concourse.mybir as mybir
+from concourse.masks import make_identity
+
+BF16 = mybir.dt.bfloat16
+F32 = mybir.dt.float32
+I32 = mybir.dt.int32
+U32 = mybir.dt.uint32
+U8 = mybir.dt.uint8
+FP8X4 = mybir.dt.float8_e4m3fn_x4
+ACT = mybir.ActivationFunctionType
+ALU = mybir.AluOpType
+
+P = 128
+PACK = 4
+IMAGES, HEIGHT, WIDTH, CHANNELS, FILTERS = 4, 16, 16, 512, 128
+PIXELS = IMAGES * HEIGHT * WIDTH
+IMAGE_PIXELS = HEIGHT * WIDTH
+PIXEL_TILES = PIXELS // P
+TILES_PER_IMAGE = IMAGE_PIXELS // P
+TILE_ROWS = P // WIDTH
+PADDED_ROWS = IMAGES * (HEIGHT + 1) + 1
+POSITIONS = 9
+WIDE_BANKS = 4
+WIDE = WIDE_BANKS * FILTERS
+OUTPUTS = 5
+SHIFTS = (0, -1, 1)
+
+FLOPS = 2 * PIXELS * POSITIONS * CHANNELS * OUTPUTS * FILTERS
+
+
+def tile_kernelception_blocka_pb_kernel(
+    tc, x, w1, w4, w6, w7, w8, out_0, out_1, out_2, out_3, out_4
+):
+    nc = tc.nc
+    wide_banks = (w1, w4, w6, w7)
+    outs = [o.rearrange("n h w f -> (n h w) f") for o in (out_0, out_1, out_2, out_3, out_4)]
+    x_rows = x.rearrange("n h w c -> (n h w) c")
+
+    with ExitStack() as stack:
+        keep = stack.enter_context(tc.tile_pool(name="keep", bufs=1))
+        psum = stack.enter_context(tc.psum_pool(name="psum", bufs=1))
+
+        identity = keep.tile([P, P], F32)
+        x_raw = keep.tile([P, PIXEL_TILES, CHANNELS], BF16)
+        x_grouped = {
+            dw: keep.tile([P, PIXELS, PACK], BF16, name="x_grouped%d" % (dw + 1), align_bytes=64)
+            for dw in SHIFTS
+        }
+        x_codes = {
+            dw: keep.tile([P, PADDED_ROWS * WIDTH], U32, name="x_codes%d" % (dw + 1), align_bytes=64)
+            for dw in SHIFTS
+        }
+        x_scales = keep.tile([P, 3, 3, PIXELS], U8, align_bytes=64)
+        wide_raw = keep.tile([P, POSITIONS, WIDE_BANKS, PACK, FILTERS], BF16)
+        wide_grouped = keep.tile([P, POSITIONS, WIDE_BANKS, FILTERS, PACK], BF16, align_bytes=64)
+        wide_codes = keep.tile([P, POSITIONS, WIDE], U32, align_bytes=64)
+        wide_scales = keep.tile([P, POSITIONS, WIDE], U8, align_bytes=64)
+        last_raw = keep.tile([P, POSITIONS, PACK, FILTERS], BF16)
+        last_grouped = keep.tile([P, POSITIONS, FILTERS, PACK], BF16, align_bytes=64)
+        last_codes = keep.tile([P, POSITIONS, FILTERS], U32, align_bytes=64)
+        last_scales = keep.tile([P, POSITIONS, FILTERS], U8, align_bytes=64)
+        squares = keep.tile([P, PIXEL_TILES, 3, FILTERS], F32)
+        results = keep.tile([P, PIXEL_TILES, OUTPUTS, FILTERS], F32)
+
+        make_identity(nc, identity[:])
+        stack.enter_context(tc.manual_schedule())
+
+        nc.vector.memset(x_scales[:].bitcast(I32), 0)
+        for dw in SHIFTS:
+            padded = x_codes[dw][:].bitcast(I32).rearrange("p (r w) -> p r w", w=WIDTH)
+            nc.vector.memset(padded[:, 0 : PADDED_ROWS : HEIGHT + 1, :], 0)
+        for dw, edge in ((-1, 0), (1, WIDTH - 1)):
+            by_column = x_grouped[dw][:].rearrange("p (r w) j -> p r w j", w=WIDTH)
+            nc.vector.memset(by_column[:, :, edge, :], 0.0)
+
+        order = [(dh, dw) for dw in SHIFTS for dh in SHIFTS]
+
+        def position(dh, dw):
+            return (dh + 1) * 3 + (dw + 1)
+
+        def load_wide(t):
+            for b, w in enumerate(wide_banks):
+                nc.sync.dma_start(
+                    out=wide_raw[:, t, b],
+                    in_=w[t * CHANNELS : (t + 1) * CHANNELS, :].rearrange("(p j) f -> p j f", j=PACK),
+                )
+
+        def load_image(n):
+            nc.sync.dma_start(
+                out=x_raw[:, n * TILES_PER_IMAGE : (n + 1) * TILES_PER_IMAGE, :],
+                in_=x_rows[n * IMAGE_PIXELS : (n + 1) * IMAGE_PIXELS, :].rearrange(
+                    "(i p) c -> p i c", p=P
+                ),
+            )
+
+        load_wide(position(*order[0]))
+        for n in range(IMAGES):
+            load_image(n)
+        for dh, dw in order[1:]:
+            load_wide(position(dh, dw))
+        nc.sync.dma_start(
+            out=last_raw[:], in_=w8.rearrange("(t p j) f -> p t j f", p=P, j=PACK)
+        )
+
+        def regroup_wide(t):
+            nc.vector.tensor_copy(
+                out=wide_grouped[:, t, 0:2].rearrange("p b (c i) j -> p b c j i", i=4),
+                in_=wide_raw[:, t, 0:2].rearrange("p b j (c i) -> p b c j i", i=4),
+            )
+            for b in (2, 3):
+                nc.scalar.copy(
+                    out=wide_grouped[:, t, b].rearrange("p (c i) j -> p c j i", i=4),
+                    in_=wide_raw[:, t, b].rearrange("p j (c i) -> p c j i", i=4),
+                )
+
+        def quantise_wide(t):
+            nc.vector.quantize_mx(
+                out=wide_codes[:, t, :].bitcast(FP8X4),
+                scales=wide_scales[:, t, :],
+                in_=wide_grouped[:, t].rearrange("p b f j -> p (b f j)"),
+            )
+
+        x_words = x_raw[:].bitcast(F32).rearrange("p i (q u) -> p i u q", u=2)
+
+        def flip_tile(i):
+            flipped = psum.tile([P, 2, P], F32, name="flipped%d" % i, tag="bank%d" % i)
+            for u in range(2):
+                nc.tensor.transpose(flipped[:, u, :], x_words[:, i, u, :], identity[:])
+            nc.scalar.copy(
+                out=x_grouped[0][:].bitcast(F32)[:, i * P : (i + 1) * P, :],
+                in_=flipped[:].rearrange("q u r -> q r u"),
+            )
+
+        def shift_pixels(dw):
+            source = x_grouped[0][:].rearrange("p (r w) j -> p r w j", w=WIDTH)
+            shifted = x_grouped[dw][:].rearrange("p (r w) j -> p r w j", w=WIDTH)
+            first, end = max(0, -dw), WIDTH - max(0, dw)
+            nc.vector.tensor_copy(
+                out=shifted[:, :, first:end, :], in_=source[:, :, first + dw : end + dw, :]
+            )
+
+        def quantise_image(dw, n):
+            first_word = (n * (HEIGHT + 1) + 1) * WIDTH
+            pixels = slice(n * IMAGE_PIXELS, (n + 1) * IMAGE_PIXELS)
+            nc.vector.quantize_mx(
+                out=x_codes[dw][:, first_word : first_word + IMAGE_PIXELS].bitcast(FP8X4),
+                scales=x_scales[:, dw + 1, 1, pixels],
+                in_=x_grouped[dw][:, pixels, :].rearrange("p r j -> p (r j)"),
+            )
+
+        def move_scales(dw):
+            planes = x_scales[:].bitcast(I32).rearrange("p a b (n c) -> p a b n c", n=IMAGES)
+            row = WIDTH // 4
+            size = IMAGE_PIXELS // 4
+            nc.vector.tensor_copy(
+                out=planes[:, dw + 1, 0, :, row:size], in_=planes[:, dw + 1, 1, :, 0 : size - row]
+            )
+            nc.vector.tensor_copy(
+                out=planes[:, dw + 1, 2, :, 0 : size - row], in_=planes[:, dw + 1, 1, :, row:size]
+            )
+
+        def pixel_window(i, dh, dw):
+            n, half = divmod(i, TILES_PER_IMAGE)
+            first_word = (n * (HEIGHT + 1) + 1 + half * TILE_ROWS + dh) * WIDTH
+            return (
+                x_codes[dw][:, first_word : first_word + P].bitcast(FP8X4),
+                x_scales[:, dw + 1, dh + 1, i * P : (i + 1) * P],
+            )
+
+        wide_sums = []
+
+        def multiply_wide(s):
+            dh, dw = order[s]
+            t = position(dh, dw)
+            for i in range(PIXEL_TILES):
+                if s == 0:
+                    wide_sums.append(psum.tile([P, WIDE], F32, name="wide_sum%d" % i, tag="bank%d" % i))
+                codes, scales = pixel_window(i, dh, dw)
+                nc.tensor.matmul_mx(
+                    out=wide_sums[i][:],
+                    lhsT=codes,
+                    lhsT_scale=scales,
+                    rhs=wide_codes[:, t, :].bitcast(FP8X4),
+                    rhs_scale=wide_scales[:, t, :],
+                    start=(s == 0),
+                    stop=(s == POSITIONS - 1),
+                )
+
+        def cube_of_one_plus(result, square, sums):
+            nc.scalar.activation(out=square, in_=sums, func=ACT.Square, bias=1.0, scale=1.0)
+            nc.vector.scalar_tensor_tensor(
+                out=result, in0=sums, scalar=1.0, in1=square, op0=ALU.add, op1=ALU.mult
+            )
+
+        def store(i, first_output, end_output):
+            for b in range(first_output, end_output):
+                nc.sync.dma_start(out=outs[b][i * P : (i + 1) * P, :], in_=results[:, i, b, :])
+
+        def finish_wide(i):
+            sums = wide_sums[i]
+            nc.scalar.activation(
+                out=results[:, i, 1, :], in_=sums[:, FILTERS : 2 * FILTERS], func=ACT.Tanh
+            )
+            cube_of_one_plus(
+                results[:, i, 2:4, :].rearrange("p b f -> p (b f)"),
+                squares[:, i, 0:2, :].rearrange("p b f -> p (b f)"),
+                sums[:, 2 * FILTERS : 4 * FILTERS],
+            )
+            nc.vector.tensor_copy(out=results[:, i, 0, :], in_=sums[:, 0:FILTERS])
+            store(i, 0, 4)
+
+        last_sums = []
+
+        def multiply_last(i):
+            last_sums.append(psum.tile([P, FILTERS], F32, name="last_sum%d" % i, tag="bank%d" % i))
+            for s, (dh, dw) in enumerate(order):
+                t = position(dh, dw)
+                codes, scales = pixel_window(i, dh, dw)
+                nc.tensor.matmul_mx(
+                    out=last_sums[i][:],
+                    lhsT=codes,
+                    lhsT_scale=scales,
+                    rhs=last_codes[:, t, :].bitcast(FP8X4),
+                    rhs_scale=last_scales[:, t, :],
+                    start=(s == 0),
+                    stop=(s == POSITIONS - 1),
+                )
+
+        def finish_last(i):
+            cube_of_one_plus(results[:, i, 4, :], squares[:, i, 2, :], last_sums[i][:])
+            store(i, 4, 5)
+
+        regroup_wide(position(*order[0]))
+        for i in range(PIXEL_TILES):
+            flip_tile(i)
+        quantise_wide(position(*order[0]))
+        for n in range(IMAGES):
+            quantise_image(0, n)
+        move_scales(0)
+        multiply_wide(0)
+
+        for s in range(1, POSITIONS):
+            t = position(*order[s])
+            group, step = divmod(s - 1, 3)
+            regroup_wide(t)
+            if group + 1 < len(SHIFTS) and step == 0:
+                shift_pixels(SHIFTS[group + 1])
+            quantise_wide(t)
+            if group + 1 < len(SHIFTS) and step == 1:
+                for n in range(IMAGES):
+                    quantise_image(SHIFTS[group + 1], n)
+                move_scales(SHIFTS[group + 1])
+            multiply_wide(s)
+
+        for t in range(POSITIONS):
+            copy = nc.vector.tensor_copy if t % 2 == 0 else nc.scalar.copy
+            copy(
+                out=last_grouped[:, t].rearrange("p (c i) j -> p c j i", i=4),
+                in_=last_raw[:, t].rearrange("p j (c i) -> p c j i", i=4),
+            )
+        for t in range(POSITIONS):
+            nc.vector.quantize_mx(
+                out=last_codes[:, t, :].bitcast(FP8X4),
+                scales=last_scales[:, t, :],
+                in_=last_grouped[:, t].rearrange("p f j -> p (f j)"),
+            )
+
+        for i in range(PIXEL_TILES):
+            finish_wide(i)
+            multiply_last(i)
+        for i in range(PIXEL_TILES):
+            finish_last(i)

@@ -16,16 +16,18 @@ P = 128
 PACK = 4
 IMAGES, HEIGHT, WIDTH, CHANNELS, FILTERS = 4, 16, 16, 512, 128
 PIXELS = IMAGES * HEIGHT * WIDTH
-IMAGE_PIXELS = HEIGHT * WIDTH
+ROW = WIDTH * IMAGES
+PADDED = (HEIGHT + 2) * ROW
 PIXEL_TILES = PIXELS // P
-TILES_PER_IMAGE = IMAGE_PIXELS // P
-TILE_ROWS = P // WIDTH
-PADDED_ROWS = IMAGES * (HEIGHT + 1) + 1
+TILE_ROWS = P // ROW
+STRIP = TILE_ROWS * WIDTH
 POSITIONS = 9
 WIDE_BANKS = 4
 WIDE = WIDE_BANKS * FILTERS
 OUTPUTS = 5
 SHIFTS = (0, -1, 1)
+STREAMED = 6
+STORE_TILES = 4
 
 FLOPS = 2 * PIXELS * POSITIONS * CHANNELS * OUTPUTS * FILTERS
 
@@ -35,8 +37,10 @@ def tile_kernelception_blocka_pb_kernel(
 ):
     nc = tc.nc
     wide_banks = (w1, w4, w6, w7)
-    outs = [o.rearrange("n h w f -> (n h w) f") for o in (out_0, out_1, out_2, out_3, out_4)]
-    x_rows = x.rearrange("n h w c -> (n h w) c")
+    outs = (out_0, out_1, out_2, out_3, out_4)
+
+    def strips(image):
+        return image.rearrange("h w c -> (h w) c").rearrange("(i a) c -> a i c", a=STRIP)
 
     with ExitStack() as stack:
         keep = stack.enter_context(tc.tile_pool(name="keep", bufs=1))
@@ -44,15 +48,9 @@ def tile_kernelception_blocka_pb_kernel(
 
         identity = keep.tile([P, P], F32)
         x_raw = keep.tile([P, PIXEL_TILES, CHANNELS], BF16)
-        x_grouped = {
-            dw: keep.tile([P, PIXELS, PACK], BF16, name="x_grouped%d" % (dw + 1), align_bytes=64)
-            for dw in SHIFTS
-        }
-        x_codes = {
-            dw: keep.tile([P, PADDED_ROWS * WIDTH], U32, name="x_codes%d" % (dw + 1), align_bytes=64)
-            for dw in SHIFTS
-        }
-        x_scales = keep.tile([P, 3, 3, PIXELS], U8, align_bytes=64)
+        x_grouped = keep.tile([P, PIXELS, PACK], BF16, align_bytes=64)
+        x_codes = keep.tile([P, len(SHIFTS), PADDED], U32, align_bytes=64)
+        x_scales = keep.tile([P, len(SHIFTS), PADDED], U8, align_bytes=64)
         wide_raw = keep.tile([P, POSITIONS, WIDE_BANKS, PACK, FILTERS], BF16)
         wide_grouped = keep.tile([P, POSITIONS, WIDE_BANKS, FILTERS, PACK], BF16, align_bytes=64)
         wide_codes = keep.tile([P, POSITIONS, WIDE], U32, align_bytes=64)
@@ -67,13 +65,8 @@ def tile_kernelception_blocka_pb_kernel(
         make_identity(nc, identity[:])
         stack.enter_context(tc.manual_schedule())
 
+        nc.vector.memset(x_codes[:].bitcast(I32), 0)
         nc.vector.memset(x_scales[:].bitcast(I32), 0)
-        for dw in SHIFTS:
-            padded = x_codes[dw][:].bitcast(I32).rearrange("p (r w) -> p r w", w=WIDTH)
-            nc.vector.memset(padded[:, 0 : PADDED_ROWS : HEIGHT + 1, :], 0)
-        for dw, edge in ((-1, 0), (1, WIDTH - 1)):
-            by_column = x_grouped[dw][:].rearrange("p (r w) j -> p r w j", w=WIDTH)
-            nc.vector.memset(by_column[:, :, edge, :], 0.0)
 
         order = [(dh, dw) for dw in SHIFTS for dh in SHIFTS]
 
@@ -87,22 +80,16 @@ def tile_kernelception_blocka_pb_kernel(
                     in_=w[t * CHANNELS : (t + 1) * CHANNELS, :].rearrange("(p j) f -> p j f", j=PACK),
                 )
 
-        def load_image(n):
-            nc.sync.dma_start(
-                out=x_raw[:, n * TILES_PER_IMAGE : (n + 1) * TILES_PER_IMAGE, :],
-                in_=x_rows[n * IMAGE_PIXELS : (n + 1) * IMAGE_PIXELS, :].rearrange(
-                    "(i p) c -> p i c", p=P
-                ),
-            )
+        def load_pixels(tiles):
+            for n in range(IMAGES):
+                nc.sync.dma_start(out=x_raw[n:P:IMAGES, tiles, :], in_=strips(x[n])[:, tiles, :])
 
         load_wide(position(*order[0]))
-        for n in range(IMAGES):
-            load_image(n)
+        load_pixels(slice(0, PIXEL_TILES // 2))
+        load_pixels(slice(PIXEL_TILES // 2, PIXEL_TILES))
         for dh, dw in order[1:]:
             load_wide(position(dh, dw))
-        nc.sync.dma_start(
-            out=last_raw[:], in_=w8.rearrange("(t p j) f -> p t j f", p=P, j=PACK)
-        )
+        nc.sync.dma_start(out=last_raw[:], in_=w8.rearrange("(t p j) f -> p t j f", p=P, j=PACK))
 
         def regroup_wide(t):
             nc.vector.tensor_copy(
@@ -129,74 +116,56 @@ def tile_kernelception_blocka_pb_kernel(
             for u in range(2):
                 nc.tensor.transpose(flipped[:, u, :], x_words[:, i, u, :], identity[:])
             nc.scalar.copy(
-                out=x_grouped[0][:].bitcast(F32)[:, i * P : (i + 1) * P, :],
+                out=x_grouped[:].bitcast(F32)[:, i * P : (i + 1) * P, :],
                 in_=flipped[:].rearrange("q u r -> q r u"),
             )
 
-        def shift_pixels(dw):
-            source = x_grouped[0][:].rearrange("p (r w) j -> p r w j", w=WIDTH)
-            shifted = x_grouped[dw][:].rearrange("p (r w) j -> p r w j", w=WIDTH)
-            first, end = max(0, -dw), WIDTH - max(0, dw)
-            nc.vector.tensor_copy(
-                out=shifted[:, :, first:end, :], in_=source[:, :, first + dw : end + dw, :]
-            )
-
-        def quantise_image(dw, n):
-            first_word = (n * (HEIGHT + 1) + 1) * WIDTH
-            pixels = slice(n * IMAGE_PIXELS, (n + 1) * IMAGE_PIXELS)
+        def quantise_pixels(first_tile, tiles):
             nc.vector.quantize_mx(
-                out=x_codes[dw][:, first_word : first_word + IMAGE_PIXELS].bitcast(FP8X4),
-                scales=x_scales[:, dw + 1, 1, pixels],
-                in_=x_grouped[dw][:, pixels, :].rearrange("p r j -> p (r j)"),
+                out=x_codes[:, 0, ROW + first_tile * P : ROW + (first_tile + tiles) * P].bitcast(FP8X4),
+                scales=x_scales[:, 0, ROW + first_tile * P : ROW + (first_tile + tiles) * P],
+                in_=x_grouped[:, first_tile * P : (first_tile + tiles) * P, :].rearrange(
+                    "p r j -> p (r j)"
+                ),
             )
 
-        def move_scales(dw):
-            planes = x_scales[:].bitcast(I32).rearrange("p a b (n c) -> p a b n c", n=IMAGES)
-            row = WIDTH // 4
-            size = IMAGE_PIXELS // 4
-            nc.vector.tensor_copy(
-                out=planes[:, dw + 1, 0, :, row:size], in_=planes[:, dw + 1, 1, :, 0 : size - row]
-            )
-            nc.vector.tensor_copy(
-                out=planes[:, dw + 1, 2, :, 0 : size - row], in_=planes[:, dw + 1, 1, :, row:size]
-            )
+        def move_pixels(g):
+            dw = SHIFTS[g]
+            for plane, pixel in ((x_codes, IMAGES), (x_scales, IMAGES // 4)):
+                rows = plane[:].bitcast(I32).rearrange("p g (r c) -> p g r c", r=HEIGHT + 2)
+                first, end = max(0, -dw) * pixel, (WIDTH - max(0, dw)) * pixel
+                nc.vector.tensor_copy(
+                    out=rows[:, g, 1 : HEIGHT + 1, first:end],
+                    in_=rows[:, 0, 1 : HEIGHT + 1, first + dw * pixel : end + dw * pixel],
+                )
 
         def pixel_window(i, dh, dw):
-            n, half = divmod(i, TILES_PER_IMAGE)
-            first_word = (n * (HEIGHT + 1) + 1 + half * TILE_ROWS + dh) * WIDTH
-            return (
-                x_codes[dw][:, first_word : first_word + P].bitcast(FP8X4),
-                x_scales[:, dw + 1, dh + 1, i * P : (i + 1) * P],
-            )
+            g = SHIFTS.index(dw)
+            first = (i * TILE_ROWS + 1 + dh) * ROW
+            return x_codes[:, g, first : first + P].bitcast(FP8X4), x_scales[:, g, first : first + P]
 
-        wide_sums = []
+        wide_sums = [None] * PIXEL_TILES
+        last_sums = [None] * PIXEL_TILES
 
-        def multiply_wide(s):
+        def multiply(sums, i, s, w_codes, w_scales):
             dh, dw = order[s]
             t = position(dh, dw)
-            for i in range(PIXEL_TILES):
-                if s == 0:
-                    wide_sums.append(psum.tile([P, WIDE], F32, name="wide_sum%d" % i, tag="bank%d" % i))
-                codes, scales = pixel_window(i, dh, dw)
-                nc.tensor.matmul_mx(
-                    out=wide_sums[i][:],
-                    lhsT=codes,
-                    lhsT_scale=scales,
-                    rhs=wide_codes[:, t, :].bitcast(FP8X4),
-                    rhs_scale=wide_scales[:, t, :],
-                    start=(s == 0),
-                    stop=(s == POSITIONS - 1),
-                )
+            codes, scales = pixel_window(i, dh, dw)
+            nc.tensor.matmul_mx(
+                out=sums,
+                lhsT=codes,
+                lhsT_scale=scales,
+                rhs=w_codes[:, t, :].bitcast(FP8X4),
+                rhs_scale=w_scales[:, t, :],
+                start=(s == 0),
+                stop=(s == POSITIONS - 1),
+            )
 
         def cube_of_one_plus(result, square, sums):
             nc.scalar.activation(out=square, in_=sums, func=ACT.Square, bias=1.0, scale=1.0)
             nc.vector.scalar_tensor_tensor(
                 out=result, in0=sums, scalar=1.0, in1=square, op0=ALU.add, op1=ALU.mult
             )
-
-        def store(i, first_output, end_output):
-            for b in range(first_output, end_output):
-                nc.sync.dma_start(out=outs[b][i * P : (i + 1) * P, :], in_=results[:, i, b, :])
 
         def finish_wide(i):
             sums = wide_sums[i]
@@ -209,50 +178,37 @@ def tile_kernelception_blocka_pb_kernel(
                 sums[:, 2 * FILTERS : 4 * FILTERS],
             )
             nc.vector.tensor_copy(out=results[:, i, 0, :], in_=sums[:, 0:FILTERS])
-            store(i, 0, 4)
-
-        last_sums = []
-
-        def multiply_last(i):
-            last_sums.append(psum.tile([P, FILTERS], F32, name="last_sum%d" % i, tag="bank%d" % i))
-            for s, (dh, dw) in enumerate(order):
-                t = position(dh, dw)
-                codes, scales = pixel_window(i, dh, dw)
-                nc.tensor.matmul_mx(
-                    out=last_sums[i][:],
-                    lhsT=codes,
-                    lhsT_scale=scales,
-                    rhs=last_codes[:, t, :].bitcast(FP8X4),
-                    rhs_scale=last_scales[:, t, :],
-                    start=(s == 0),
-                    stop=(s == POSITIONS - 1),
-                )
 
         def finish_last(i):
             cube_of_one_plus(results[:, i, 4, :], squares[:, i, 2, :], last_sums[i][:])
-            store(i, 4, 5)
+
+        def store(last_tile, banks):
+            if (last_tile + 1) % STORE_TILES == 0:
+                tiles = slice(last_tile + 1 - STORE_TILES, last_tile + 1)
+                for b in banks:
+                    for n in range(IMAGES):
+                        nc.sync.dma_start(
+                            out=strips(outs[b][n])[:, tiles, :], in_=results[n:P:IMAGES, tiles, b, :]
+                        )
 
         regroup_wide(position(*order[0]))
         for i in range(PIXEL_TILES):
             flip_tile(i)
         quantise_wide(position(*order[0]))
-        for n in range(IMAGES):
-            quantise_image(0, n)
-        move_scales(0)
-        multiply_wide(0)
+        for i in range(0, PIXEL_TILES, 2):
+            quantise_pixels(i, 2)
 
-        for s in range(1, POSITIONS):
-            t = position(*order[s])
-            group, step = divmod(s - 1, 3)
-            regroup_wide(t)
-            if group + 1 < len(SHIFTS) and step == 0:
-                shift_pixels(SHIFTS[group + 1])
-            quantise_wide(t)
-            if group + 1 < len(SHIFTS) and step == 1:
-                for n in range(IMAGES):
-                    quantise_image(SHIFTS[group + 1], n)
-                move_scales(SHIFTS[group + 1])
-            multiply_wide(s)
+        for s in range(POSITIONS):
+            if s > 0:
+                regroup_wide(position(*order[s]))
+                if (s + 1) % 3 == 0 and s + 1 < POSITIONS:
+                    move_pixels((s + 1) // 3)
+                quantise_wide(position(*order[s]))
+            if s < STREAMED:
+                for i in range(PIXEL_TILES):
+                    if s == 0:
+                        wide_sums[i] = psum.tile([P, WIDE], F32, name="wide_sum%d" % i, tag="bank%d" % i)
+                    multiply(wide_sums[i][:], i, s, wide_codes, wide_scales)
 
         for t in range(POSITIONS):
             copy = nc.vector.tensor_copy if t % 2 == 0 else nc.scalar.copy
@@ -268,7 +224,13 @@ def tile_kernelception_blocka_pb_kernel(
             )
 
         for i in range(PIXEL_TILES):
+            for s in range(STREAMED, POSITIONS):
+                multiply(wide_sums[i][:], i, s, wide_codes, wide_scales)
             finish_wide(i)
-            multiply_last(i)
+            store(i, range(WIDE_BANKS))
         for i in range(PIXEL_TILES):
+            last_sums[i] = psum.tile([P, FILTERS], F32, name="last_sum%d" % i, tag="bank%d" % i)
+            for s in range(POSITIONS):
+                multiply(last_sums[i][:], i, s, last_codes, last_scales)
             finish_last(i)
+            store(i, range(WIDE_BANKS, OUTPUTS))

@@ -28,6 +28,9 @@ OUTPUTS = 5
 SHIFTS = (0, -1, 1)
 STREAMED = 6
 STORE_TILES = 4
+SLAB_ROWS = P // WIDTH
+HALVES = HEIGHT // SLAB_ROWS
+PAIR = 2
 
 FLOPS = 2 * PIXELS * POSITIONS * CHANNELS * OUTPUTS * FILTERS
 
@@ -47,7 +50,7 @@ def tile_kernelception_blocka_pb_kernel(
         psum = stack.enter_context(tc.psum_pool(name="psum", bufs=1))
 
         identity = keep.tile([P, P], F32)
-        x_raw = keep.tile([P, PIXEL_TILES, CHANNELS], BF16)
+        x_raw = keep.tile([P, HALVES, IMAGES, CHANNELS], BF16)
         x_grouped = keep.tile([P, PIXELS, PACK], BF16, align_bytes=64)
         x_codes = keep.tile([P, len(SHIFTS), PADDED], U32, align_bytes=64)
         x_scales = keep.tile([P, len(SHIFTS), PADDED], U8, align_bytes=64)
@@ -80,13 +83,16 @@ def tile_kernelception_blocka_pb_kernel(
                     in_=w[t * CHANNELS : (t + 1) * CHANNELS, :].rearrange("(p j) f -> p j f", j=PACK),
                 )
 
-        def load_pixels(tiles):
-            for n in range(IMAGES):
-                nc.sync.dma_start(out=x_raw[n:P:IMAGES, tiles, :], in_=strips(x[n])[:, tiles, :])
+        slabs = x.rearrange("n (b r) w c -> (r w) b n c", b=HALVES)
+
+        def load_pixels(half, first_image):
+            images = slice(first_image, first_image + PAIR)
+            nc.sync.dma_start(out=x_raw[:, half, images, :], in_=slabs[:, half, images, :])
 
         load_wide(position(*order[0]))
-        load_pixels(slice(0, PIXEL_TILES // 2))
-        load_pixels(slice(PIXEL_TILES // 2, PIXEL_TILES))
+        for half in range(HALVES):
+            for first_image in range(0, IMAGES, PAIR):
+                load_pixels(half, first_image)
         for dh, dw in order[1:]:
             load_wide(position(dh, dw))
         nc.sync.dma_start(out=last_raw[:], in_=w8.rearrange("(t p j) f -> p t j f", p=P, j=PACK))
@@ -109,15 +115,20 @@ def tile_kernelception_blocka_pb_kernel(
                 in_=wide_grouped[:, t].rearrange("p b f j -> p (b f j)"),
             )
 
-        x_words = x_raw[:].bitcast(F32).rearrange("p i (q u) -> p i u q", u=2)
+        x_words = x_raw[:].bitcast(F32).rearrange("p b n (q u) -> p b n u q", u=2)
+        grouped_words = x_grouped[:].bitcast(F32).rearrange("q (b r n) u -> q b r n u", b=HALVES, n=IMAGES)
 
-        def flip_tile(i):
-            flipped = psum.tile([P, 2, P], F32, name="flipped%d" % i, tag="bank%d" % i)
-            for u in range(2):
-                nc.tensor.transpose(flipped[:, u, :], x_words[:, i, u, :], identity[:])
+        def flip_pair(half, first_image):
+            bank = PIXEL_TILES - 1 - (half * IMAGES + first_image) // PAIR
+            flipped = psum.tile([P, PAIR, 2, P], F32, name="flipped%d" % bank, tag="bank%d" % bank)
+            for m in range(PAIR):
+                for u in range(2):
+                    nc.tensor.transpose(
+                        flipped[:, m, u, :], x_words[:, half, first_image + m, u, :], identity[:]
+                    )
             nc.scalar.copy(
-                out=x_grouped[:].bitcast(F32)[:, i * P : (i + 1) * P, :],
-                in_=flipped[:].rearrange("q u r -> q r u"),
+                out=grouped_words[:, half, :, first_image : first_image + PAIR, :],
+                in_=flipped[:].rearrange("q m u r -> q r m u"),
             )
 
         def quantise_pixels(first_tile, tiles):
@@ -192,8 +203,9 @@ def tile_kernelception_blocka_pb_kernel(
                         )
 
         regroup_wide(position(*order[0]))
-        for i in range(PIXEL_TILES):
-            flip_tile(i)
+        for half in range(HALVES):
+            for first_image in range(0, IMAGES, PAIR):
+                flip_pair(half, first_image)
         quantise_wide(position(*order[0]))
         for i in range(0, PIXEL_TILES, 2):
             quantise_pixels(i, 2)

from contextlib import ExitStack

import concourse.mybir as mybir
from concourse.masks import make_identity

BF16 = mybir.dt.bfloat16
F32 = mybir.dt.float32
I32 = mybir.dt.int32
U32 = mybir.dt.uint32
U8 = mybir.dt.uint8
FP8X4 = mybir.dt.float8_e4m3fn_x4
ACT = mybir.ActivationFunctionType
ALU = mybir.AluOpType

P = 128
PACK = 4
IMAGES, HEIGHT, WIDTH, CHANNELS, FILTERS = 4, 16, 16, 512, 128
PIXELS = IMAGES * HEIGHT * WIDTH
ROW = WIDTH * IMAGES
PADDED = (HEIGHT + 2) * ROW
PIXEL_TILES = PIXELS // P
TILE_ROWS = P // ROW
STRIP = TILE_ROWS * WIDTH
POSITIONS = 9
WIDE_BANKS = 4
WIDE = WIDE_BANKS * FILTERS
OUTPUTS = 5
SHIFTS = (0, -1, 1)
STREAMED = 6
STORE_TILES = 4
SLAB_ROWS = P // WIDTH
HALVES = HEIGHT // SLAB_ROWS
PAIR = 2

FLOPS = 2 * PIXELS * POSITIONS * CHANNELS * OUTPUTS * FILTERS


def tile_kernelception_blocka_pb_kernel(
    tc, x, w1, w4, w6, w7, w8, out_0, out_1, out_2, out_3, out_4
):
    nc = tc.nc
    wide_banks = (w1, w4, w6, w7)
    outs = (out_0, out_1, out_2, out_3, out_4)

    def strips(image):
        return image.rearrange("h w c -> (h w) c").rearrange("(i a) c -> a i c", a=STRIP)

    with ExitStack() as stack:
        keep = stack.enter_context(tc.tile_pool(name="keep", bufs=1))
        psum = stack.enter_context(tc.psum_pool(name="psum", bufs=1))

        identity = keep.tile([P, P], F32)
        x_raw = keep.tile([P, HALVES, IMAGES, CHANNELS], BF16)
        x_grouped = keep.tile([P, PIXELS, PACK], BF16, align_bytes=64)
        x_codes = keep.tile([P, len(SHIFTS), PADDED], U32, align_bytes=64)
        x_scales = keep.tile([P, len(SHIFTS), PADDED], U8, align_bytes=64)
        wide_raw = keep.tile([P, POSITIONS, WIDE_BANKS, PACK, FILTERS], BF16)
        wide_grouped = keep.tile([P, POSITIONS, WIDE_BANKS, FILTERS, PACK], BF16, align_bytes=64)
        wide_codes = keep.tile([P, POSITIONS, WIDE], U32, align_bytes=64)
        wide_scales = keep.tile([P, POSITIONS, WIDE], U8, align_bytes=64)
        last_raw = keep.tile([P, POSITIONS, PACK, FILTERS], BF16)
        last_grouped = keep.tile([P, POSITIONS, FILTERS, PACK], BF16, align_bytes=64)
        last_codes = keep.tile([P, POSITIONS, FILTERS], U32, align_bytes=64)
        last_scales = keep.tile([P, POSITIONS, FILTERS], U8, align_bytes=64)
        squares = keep.tile([P, PIXEL_TILES, 3, FILTERS], F32)
        results = keep.tile([P, PIXEL_TILES, OUTPUTS, FILTERS], F32)

        make_identity(nc, identity[:])
        stack.enter_context(tc.manual_schedule())

        nc.vector.memset(x_codes[:].bitcast(I32), 0)
        nc.vector.memset(x_scales[:].bitcast(I32), 0)

        order = [(dh, dw) for dw in SHIFTS for dh in SHIFTS]

        def position(dh, dw):
            return (dh + 1) * 3 + (dw + 1)

        def load_wide(t):
            for b, w in enumerate(wide_banks):
                nc.sync.dma_start(
                    out=wide_raw[:, t, b],
                    in_=w[t * CHANNELS : (t + 1) * CHANNELS, :].rearrange("(p j) f -> p j f", j=PACK),
                )

        slabs = x.rearrange("n (b r) w c -> (r w) b n c", b=HALVES)

        def load_pixels(half, first_image):
            images = slice(first_image, first_image + PAIR)
            nc.sync.dma_start(out=x_raw[:, half, images, :], in_=slabs[:, half, images, :])

        load_wide(position(*order[0]))
        for half in range(HALVES):
            for first_image in range(0, IMAGES, PAIR):
                load_pixels(half, first_image)
        for dh, dw in order[1:]:
            load_wide(position(dh, dw))
        nc.sync.dma_start(out=last_raw[:], in_=w8.rearrange("(t p j) f -> p t j f", p=P, j=PACK))

        def regroup_wide(t):
            nc.vector.tensor_copy(
                out=wide_grouped[:, t, 0:2].rearrange("p b (c i) j -> p b c j i", i=4),
                in_=wide_raw[:, t, 0:2].rearrange("p b j (c i) -> p b c j i", i=4),
            )
            for b in (2, 3):
                nc.scalar.copy(
                    out=wide_grouped[:, t, b].rearrange("p (c i) j -> p c j i", i=4),
                    in_=wide_raw[:, t, b].rearrange("p j (c i) -> p c j i", i=4),
                )

        def quantise_wide(t):
            nc.vector.quantize_mx(
                out=wide_codes[:, t, :].bitcast(FP8X4),
                scales=wide_scales[:, t, :],
                in_=wide_grouped[:, t].rearrange("p b f j -> p (b f j)"),
            )

        x_words = x_raw[:].bitcast(F32).rearrange("p b n (q u) -> p b n u q", u=2)
        grouped_words = x_grouped[:].bitcast(F32).rearrange("q (b r n) u -> q b r n u", b=HALVES, n=IMAGES)

        def flip_pair(half, first_image):
            bank = PIXEL_TILES - 1 - (half * IMAGES + first_image) // PAIR
            flipped = psum.tile([P, PAIR, 2, P], F32, name="flipped%d" % bank, tag="bank%d" % bank)
            for m in range(PAIR):
                for u in range(2):
                    nc.tensor.transpose(
                        flipped[:, m, u, :], x_words[:, half, first_image + m, u, :], identity[:]
                    )
            nc.scalar.copy(
                out=grouped_words[:, half, :, first_image : first_image + PAIR, :],
                in_=flipped[:].rearrange("q m u r -> q r m u"),
            )

        def quantise_pixels(first_tile, tiles):
            nc.vector.quantize_mx(
                out=x_codes[:, 0, ROW + first_tile * P : ROW + (first_tile + tiles) * P].bitcast(FP8X4),
                scales=x_scales[:, 0, ROW + first_tile * P : ROW + (first_tile + tiles) * P],
                in_=x_grouped[:, first_tile * P : (first_tile + tiles) * P, :].rearrange(
                    "p r j -> p (r j)"
                ),
            )

        def move_pixels(g):
            dw = SHIFTS[g]
            for plane, pixel in ((x_codes, IMAGES), (x_scales, IMAGES // 4)):
                rows = plane[:].bitcast(I32).rearrange("p g (r c) -> p g r c", r=HEIGHT + 2)
                first, end = max(0, -dw) * pixel, (WIDTH - max(0, dw)) * pixel
                nc.vector.tensor_copy(
                    out=rows[:, g, 1 : HEIGHT + 1, first:end],
                    in_=rows[:, 0, 1 : HEIGHT + 1, first + dw * pixel : end + dw * pixel],
                )

        def pixel_window(i, dh, dw):
            g = SHIFTS.index(dw)
            first = (i * TILE_ROWS + 1 + dh) * ROW
            return x_codes[:, g, first : first + P].bitcast(FP8X4), x_scales[:, g, first : first + P]

        wide_sums = [None] * PIXEL_TILES
        last_sums = [None] * PIXEL_TILES

        def multiply(sums, i, s, w_codes, w_scales):
            dh, dw = order[s]
            t = position(dh, dw)
            codes, scales = pixel_window(i, dh, dw)
            nc.tensor.matmul_mx(
                out=sums,
                lhsT=codes,
                lhsT_scale=scales,
                rhs=w_codes[:, t, :].bitcast(FP8X4),
                rhs_scale=w_scales[:, t, :],
                start=(s == 0),
                stop=(s == POSITIONS - 1),
            )

        def cube_of_one_plus(result, square, sums):
            nc.scalar.activation(out=square, in_=sums, func=ACT.Square, bias=1.0, scale=1.0)
            nc.vector.scalar_tensor_tensor(
                out=result, in0=sums, scalar=1.0, in1=square, op0=ALU.add, op1=ALU.mult
            )

        def finish_wide(i):
            sums = wide_sums[i]
            nc.scalar.activation(
                out=results[:, i, 1, :], in_=sums[:, FILTERS : 2 * FILTERS], func=ACT.Tanh
            )
            cube_of_one_plus(
                results[:, i, 2:4, :].rearrange("p b f -> p (b f)"),
                squares[:, i, 0:2, :].rearrange("p b f -> p (b f)"),
                sums[:, 2 * FILTERS : 4 * FILTERS],
            )
            nc.vector.tensor_copy(out=results[:, i, 0, :], in_=sums[:, 0:FILTERS])

        def finish_last(i):
            cube_of_one_plus(results[:, i, 4, :], squares[:, i, 2, :], last_sums[i][:])

        def store(last_tile, banks):
            if (last_tile + 1) % STORE_TILES == 0:
                tiles = slice(last_tile + 1 - STORE_TILES, last_tile + 1)
                for b in banks:
                    for n in range(IMAGES):
                        nc.sync.dma_start(
                            out=strips(outs[b][n])[:, tiles, :], in_=results[n:P:IMAGES, tiles, b, :]
                        )

        regroup_wide(position(*order[0]))
        for half in range(HALVES):
            for first_image in range(0, IMAGES, PAIR):
                flip_pair(half, first_image)
        quantise_wide(position(*order[0]))
        for i in range(0, PIXEL_TILES, 2):
            quantise_pixels(i, 2)

        for s in range(POSITIONS):
            if s > 0:
                regroup_wide(position(*order[s]))
                if (s + 1) % 3 == 0 and s + 1 < POSITIONS:
                    move_pixels((s + 1) // 3)
                quantise_wide(position(*order[s]))
            if s < STREAMED:
                for i in range(PIXEL_TILES):
                    if s == 0:
                        wide_sums[i] = psum.tile([P, WIDE], F32, name="wide_sum%d" % i, tag="bank%d" % i)
                    multiply(wide_sums[i][:], i, s, wide_codes, wide_scales)

        for t in range(POSITIONS):
            copy = nc.vector.tensor_copy if t % 2 == 0 else nc.scalar.copy
            copy(
                out=last_grouped[:, t].rearrange("p (c i) j -> p c j i", i=4),
                in_=last_raw[:, t].rearrange("p j (c i) -> p c j i", i=4),
            )
        for t in range(POSITIONS):
            nc.vector.quantize_mx(
                out=last_codes[:, t, :].bitcast(FP8X4),
                scales=last_scales[:, t, :],
                in_=last_grouped[:, t].rearrange("p f j -> p (f j)"),
            )

        for i in range(PIXEL_TILES):
            for s in range(STREAMED, POSITIONS):
                multiply(wide_sums[i][:], i, s, wide_codes, wide_scales)
            finish_wide(i)
            store(i, range(WIDE_BANKS))
        for i in range(PIXEL_TILES):
            last_sums[i] = psum.tile([P, FILTERS], F32, name="last_sum%d" % i, tag="bank%d" % i)
            for s in range(POSITIONS):
                multiply(last_sums[i][:], i, s, last_codes, last_scales)
            finish_last(i)
            store(i, range(WIDE_BANKS, OUTPUTS))
